import numpy as np
import ml_dtypes

BF16 = ml_dtypes.bfloat16


def bf(x):
    return np.asarray(x, np.float32).astype(BF16)


def f32(x):
    return np.asarray(x, np.float32)


def f64(x):
    return np.asarray(x).astype(np.float64)


def striped(idx):
    return np.tile(idx.reshape(-1, 16).T, (8, 1))


Q, L, K, P, C, S, N = 8, 16, 3, 128, 384, 4096, 2048


def setup_inputs():
    return {"theta": f32(np.random.uniform(-2.0, 2.0, (C, S))), "offs": striped(np.random.permutation(S)[:N])}


def reference(theta, offs):
    idx = offs[:16].T.reshape(-1)
    a, b, z = (0.5 * f64(theta)[:, idx]).reshape(K, P, N)
    ca, sa = np.cos(a), np.sin(a)
    cb, sb = np.cos(b), np.sin(b)
    cz, sz = np.cos(z), np.sin(z)
    u00r = cz * cb * ca + sz * sb * sa
    u00i = cz * sb * sa - sz * cb * ca
    u10r = cz * sb * ca + sz * cb * sa
    u10i = sz * sb * ca - cz * cb * sa
    return np.concatenate([u00r, u00i, u10r, u10i], axis=0)

@@ -1,0 +1,73 @@
+import math
+
+import concourse.mybir as mybir
+
+F32 = mybir.dt.float32
+U16 = mybir.dt.uint16
+COPY = mybir.ActivationFunctionType.Copy
+SINE = mybir.ActivationFunctionType.Sin
+MULT = mybir.AluOpType.mult
+ADD = mybir.AluOpType.add
+SUBTRACT = mybir.AluOpType.subtract
+
+GATES = 128
+POSITIONS = 4096
+LISTED = 2048
+PIECE = 512
+COS, SIN = 0, 1
+
+
+def tile_quantumlearnablepositionalencoding_kernel(tc, theta, offs, out):
+    nc = tc.nc
+    out_blocks = out.rearrange("(q p) n -> p q n", p=GATES)
+
+    with (
+        tc.tile_pool(name="held", bufs=1) as held,
+        tc.tile_pool(name="work", bufs=2) as work,
+    ):
+        offsets = held.tile([GATES, LISTED // 16], U16, name="offsets")
+        nc.sync.dma_start(offsets[:], offs)
+
+        tables = []
+        for k, axis in enumerate("xyz"):
+            table = held.tile([GATES, POSITIONS], F32, name=f"table_{axis}")
+            nc.sync.dma_start(table[:], theta[k * GATES : (k + 1) * GATES, :])
+            tables.append(table)
+
+        quarter_turn = held.tile([GATES, 1], F32, name="quarter_turn")
+        nc.vector.memset(quarter_turn[:], math.pi / 2)
+
+        for j in range(LISTED // PIECE):
+            piece_offsets = offsets[:, j * (PIECE // 16) : (j + 1) * (PIECE // 16)]
+
+            cos_sin = []
+            for axis, table in zip("xyz", tables):
+                angle = work.tile([GATES, PIECE], F32, name=f"angle_{axis}")
+                nc.scalar.activation(angle[:], table[:].indirect(piece_offsets), COPY)
+                both = work.tile([GATES, 2, PIECE], F32, name=f"cos_sin_{axis}")
+                nc.scalar.activation(both[:, COS, :], angle[:], SINE, bias=quarter_turn[:], scale=0.5)
+                nc.scalar.activation(both[:, SIN, :], angle[:], SINE, scale=0.5)
+                cos_sin.append(both)
+            of_x, of_y, of_z = cos_sin
+
+            yx = work.tile([GATES, 2, 2, PIECE], F32, name="yx")
+            nc.vector.tensor_tensor(
+                yx[:],
+                of_y[:].unsqueeze(2).to_broadcast([GATES, 2, 2, PIECE]),
+                of_x[:].unsqueeze(1).to_broadcast([GATES, 2, 2, PIECE]),
+                MULT,
+            )
+            zyx = work.tile([GATES, 2, 2, 2, PIECE], F32, name="zyx")
+            nc.vector.tensor_tensor(
+                zyx[:].rearrange("p z y x w -> p z (y x) w"),
+                of_z[:].unsqueeze(2).to_broadcast([GATES, 2, 4, PIECE]),
+                yx[:].rearrange("p y x w -> p (y x) w").unsqueeze(1).to_broadcast([GATES, 2, 4, PIECE]),
+                MULT,
+            )
+
+            column = work.tile([GATES, 4, PIECE], F32, name="column")
+            nc.vector.tensor_tensor(column[:, 0, :], zyx[:, COS, COS, COS, :], zyx[:, SIN, SIN, SIN, :], ADD)
+            nc.vector.tensor_tensor(column[:, 1, :], zyx[:, COS, SIN, SIN, :], zyx[:, SIN, COS, COS, :], SUBTRACT)
+            nc.vector.tensor_tensor(column[:, 2, :], zyx[:, COS, SIN, COS, :], zyx[:, SIN, COS, SIN, :], ADD)
+            nc.vector.tensor_tensor(column[:, 3, :], zyx[:, SIN, SIN, COS, :], zyx[:, COS, COS, SIN, :], SUBTRACT)
+            nc.sync.dma_start(out_blocks[:, :, j * PIECE : (j + 1) * PIECE], column[:])

@@ -1,6 +1,7 @@
 import math
 
 import concourse.mybir as mybir
+from concourse.masks import make_identity
 
 F32 = mybir.dt.float32
 U16 = mybir.dt.uint16
@@ -24,6 +25,7 @@ def tile_quantumlearnablepositionalencoding_kernel(tc, theta, offs, out):
     with (
         tc.tile_pool(name="held", bufs=1) as held,
         tc.tile_pool(name="work", bufs=2) as work,
+        tc.psum_pool(name="banks", bufs=2) as banks,
     ):
         offsets = held.tile([GATES, LISTED // 16], U16, name="offsets")
         nc.sync.dma_start(offsets[:], offs)
@@ -36,6 +38,8 @@ def tile_quantumlearnablepositionalencoding_kernel(tc, theta, offs, out):
 
         quarter_turn = held.tile([GATES, 1], F32, name="quarter_turn")
         nc.vector.memset(quarter_turn[:], math.pi / 2)
+        identity = held.tile([GATES, GATES], F32, name="identity")
+        make_identity(nc, identity[:])
 
         for j in range(LISTED // PIECE):
             piece_offsets = offsets[:, j * (PIECE // 16) : (j + 1) * (PIECE // 16)]
@@ -50,24 +54,27 @@ def tile_quantumlearnablepositionalencoding_kernel(tc, theta, offs, out):
                 cos_sin.append(both)
             of_x, of_y, of_z = cos_sin
 
-            yx = work.tile([GATES, 2, 2, PIECE], F32, name="yx")
-            nc.vector.tensor_tensor(
-                yx[:],
-                of_y[:].unsqueeze(2).to_broadcast([GATES, 2, 2, PIECE]),
-                of_x[:].unsqueeze(1).to_broadcast([GATES, 2, 2, PIECE]),
-                MULT,
-            )
-            zyx = work.tile([GATES, 2, 2, 2, PIECE], F32, name="zyx")
-            nc.vector.tensor_tensor(
-                zyx[:].rearrange("p z y x w -> p z (y x) w"),
-                of_z[:].unsqueeze(2).to_broadcast([GATES, 2, 4, PIECE]),
-                yx[:].rearrange("p y x w -> p (y x) w").unsqueeze(1).to_broadcast([GATES, 2, 4, PIECE]),
-                MULT,
-            )
+            xy = work.tile([GATES, 2, 2, PIECE], F32, name="xy")
+            for x in (COS, SIN):
+                x_bank = banks.tile([GATES, PIECE], F32, name=f"x_bank{x}")
+                nc.tensor.matmul(x_bank[:], identity[:], of_x[:, x, :], start=True, stop=True)
+                nc.vector.tensor_tensor(
+                    xy[:, x, :, :], x_bank[:].unsqueeze(1).to_broadcast([GATES, 2, PIECE]), of_y[:], MULT
+                )
+            zxy = work.tile([GATES, 2, 2, 2, PIECE], F32, name="zxy")
+            for z in (COS, SIN):
+                z_bank = banks.tile([GATES, PIECE], F32, name=f"z_bank{z}")
+                nc.tensor.matmul(z_bank[:], identity[:], of_z[:, z, :], start=True, stop=True)
+                nc.vector.tensor_tensor(
+                    zxy[:, z, :, :, :].rearrange("p x y w -> p (x y) w"),
+                    z_bank[:].unsqueeze(1).to_broadcast([GATES, 4, PIECE]),
+                    xy[:].rearrange("p x y w -> p (x y) w"),
+                    MULT,
+                )
 
             column = work.tile([GATES, 4, PIECE], F32, name="column")
-            nc.vector.tensor_tensor(column[:, 0, :], zyx[:, COS, COS, COS, :], zyx[:, SIN, SIN, SIN, :], ADD)
-            nc.vector.tensor_tensor(column[:, 1, :], zyx[:, COS, SIN, SIN, :], zyx[:, SIN, COS, COS, :], SUBTRACT)
-            nc.vector.tensor_tensor(column[:, 2, :], zyx[:, COS, SIN, COS, :], zyx[:, SIN, COS, SIN, :], ADD)
-            nc.vector.tensor_tensor(column[:, 3, :], zyx[:, SIN, SIN, COS, :], zyx[:, COS, COS, SIN, :], SUBTRACT)
+            nc.gpsimd.tensor_tensor(column[:, 0, :], zxy[:, COS, COS, COS, :], zxy[:, SIN, SIN, SIN, :], ADD)
+            nc.gpsimd.tensor_tensor(column[:, 1, :], zxy[:, COS, SIN, SIN, :], zxy[:, SIN, COS, COS, :], SUBTRACT)
+            nc.gpsimd.tensor_tensor(column[:, 2, :], zxy[:, COS, COS, SIN, :], zxy[:, SIN, SIN, COS, :], ADD)
+            nc.gpsimd.tensor_tensor(column[:, 3, :], zxy[:, SIN, COS, SIN, :], zxy[:, COS, SIN, COS, :], SUBTRACT)
             nc.sync.dma_start(out_blocks[:, :, j * PIECE : (j + 1) * PIECE], column[:])

@@ -20,11 +20,11 @@ COS, SIN = 0, 1
 
 def tile_quantumlearnablepositionalencoding_kernel(tc, theta, offs, out):
     nc = tc.nc
-    out_blocks = out.rearrange("(q p) n -> p q n", p=GATES)
 
     with (
         tc.tile_pool(name="held", bufs=1) as held,
-        tc.tile_pool(name="work", bufs=2) as work,
+        tc.tile_pool(name="trig", bufs=2) as trig,
+        tc.tile_pool(name="work", bufs=3) as work,
         tc.psum_pool(name="banks", bufs=2) as banks,
     ):
         offsets = held.tile([GATES, LISTED // 16], U16, name="offsets")
@@ -38,28 +38,28 @@ def tile_quantumlearnablepositionalencoding_kernel(tc, theta, offs, out):
 
         quarter_turn = held.tile([GATES, 1], F32, name="quarter_turn")
         nc.vector.memset(quarter_turn[:], math.pi / 2)
+        warm = held.tile([GATES, 1], F32, name="warm")
+        nc.scalar.activation(warm[:], quarter_turn[:], SINE)
         identity = held.tile([GATES, GATES], F32, name="identity")
         make_identity(nc, identity[:])
 
         for j in range(LISTED // PIECE):
             piece_offsets = offsets[:, j * (PIECE // 16) : (j + 1) * (PIECE // 16)]
 
-            cos_sin = []
-            for axis, table in zip("xyz", tables):
-                angle = work.tile([GATES, PIECE], F32, name=f"angle_{axis}")
-                nc.scalar.activation(angle[:], table[:].indirect(piece_offsets), COPY)
-                both = work.tile([GATES, 2, PIECE], F32, name=f"cos_sin_{axis}")
-                nc.scalar.activation(both[:, COS, :], angle[:], SINE, bias=quarter_turn[:], scale=0.5)
-                nc.scalar.activation(both[:, SIN, :], angle[:], SINE, scale=0.5)
-                cos_sin.append(both)
-            of_x, of_y, of_z = cos_sin
+            angles = trig.tile([GATES, 3, PIECE], F32, name="angles")
+            cos_sin = trig.tile([GATES, 3, 2, PIECE], F32, name="cos_sin")
+            for k, table in enumerate(tables):
+                nc.scalar.activation(angles[:, k, :], table[:].indirect(piece_offsets), COPY)
+                nc.scalar.activation(cos_sin[:, k, COS, :], angles[:, k, :], SINE, bias=quarter_turn[:], scale=0.5)
+                nc.scalar.activation(cos_sin[:, k, SIN, :], angles[:, k, :], SINE, scale=0.5)
+            of_x, of_y, of_z = cos_sin[:, 0], cos_sin[:, 1], cos_sin[:, 2]
 
             xy = work.tile([GATES, 2, 2, PIECE], F32, name="xy")
             for x in (COS, SIN):
                 x_bank = banks.tile([GATES, PIECE], F32, name=f"x_bank{x}")
                 nc.tensor.matmul(x_bank[:], identity[:], of_x[:, x, :], start=True, stop=True)
                 nc.vector.tensor_tensor(
-                    xy[:, x, :, :], x_bank[:].unsqueeze(1).to_broadcast([GATES, 2, PIECE]), of_y[:], MULT
+                    xy[:, x, :, :], x_bank[:].unsqueeze(1).to_broadcast([GATES, 2, PIECE]), of_y, MULT
                 )
             zxy = work.tile([GATES, 2, 2, 2, PIECE], F32, name="zxy")
             for z in (COS, SIN):
@@ -72,9 +72,14 @@ def tile_quantumlearnablepositionalencoding_kernel(tc, theta, offs, out):
                     MULT,
                 )
 
-            column = work.tile([GATES, 4, PIECE], F32, name="column")
-            nc.gpsimd.tensor_tensor(column[:, 0, :], zxy[:, COS, COS, COS, :], zxy[:, SIN, SIN, SIN, :], ADD)
-            nc.gpsimd.tensor_tensor(column[:, 1, :], zxy[:, COS, SIN, SIN, :], zxy[:, SIN, COS, COS, :], SUBTRACT)
-            nc.gpsimd.tensor_tensor(column[:, 2, :], zxy[:, COS, COS, SIN, :], zxy[:, SIN, SIN, COS, :], ADD)
-            nc.gpsimd.tensor_tensor(column[:, 3, :], zxy[:, SIN, COS, SIN, :], zxy[:, COS, SIN, COS, :], SUBTRACT)
-            nc.sync.dma_start(out_blocks[:, :, j * PIECE : (j + 1) * PIECE], column[:])
+            adder = nc.vector if j == LISTED // PIECE - 1 else nc.gpsimd
+            blocks = (
+                (zxy[:, COS, COS, COS, :], ADD, zxy[:, SIN, SIN, SIN, :]),
+                (zxy[:, COS, SIN, SIN, :], SUBTRACT, zxy[:, SIN, COS, COS, :]),
+                (zxy[:, COS, COS, SIN, :], ADD, zxy[:, SIN, SIN, COS, :]),
+                (zxy[:, SIN, COS, SIN, :], SUBTRACT, zxy[:, COS, SIN, COS, :]),
+            )
+            for q, (first, op, second) in enumerate(blocks):
+                block = work.tile([GATES, PIECE], F32, name=f"block{q}")
+                adder.tensor_tensor(block[:], first, second, op)
+                nc.sync.dma_start(out[q * GATES : (q + 1) * GATES, j * PIECE : (j + 1) * PIECE], block[:])

@@ -4,28 +4,38 @@ import concourse.mybir as mybir
 from concourse.masks import make_identity
 
 F32 = mybir.dt.float32
+I32 = mybir.dt.int32
 U16 = mybir.dt.uint16
 COPY = mybir.ActivationFunctionType.Copy
 SINE = mybir.ActivationFunctionType.Sin
 MULT = mybir.AluOpType.mult
 ADD = mybir.AluOpType.add
 SUBTRACT = mybir.AluOpType.subtract
+BIT_AND = mybir.AluOpType.bitwise_and
 
 GATES = 128
 POSITIONS = 4096
 LISTED = 2048
-PIECE = 512
+CHUNK = 512
+PIECE = 256
+PIECES = LISTED // PIECE
+VECTOR_ADDS = 2
+ALL_BUT_SIGN = 0x7FFFFFFF
+SUM, DIFFERENCE = 0, 1
 COS, SIN = 0, 1
+PLUS, MINUS = 0, 1
 
 
 def tile_quantumlearnablepositionalencoding_kernel(tc, theta, offs, out):
     nc = tc.nc
+    out_blocks = out.rearrange("(q r) n -> r q n", q=4)
 
     with (
         tc.tile_pool(name="held", bufs=1) as held,
-        tc.tile_pool(name="trig", bufs=2) as trig,
+        tc.tile_pool(name="chunks", bufs=LISTED // CHUNK) as chunks,
+        tc.tile_pool(name="ahead", bufs=2) as ahead,
         tc.tile_pool(name="work", bufs=3) as work,
-        tc.psum_pool(name="banks", bufs=2) as banks,
+        tc.psum_pool(name="banks", bufs=4) as banks,
     ):
         offsets = held.tile([GATES, LISTED // 16], U16, name="offsets")
         nc.sync.dma_start(offsets[:], offs)
@@ -35,51 +45,76 @@ def tile_quantumlearnablepositionalencoding_kernel(tc, theta, offs, out):
             table = held.tile([GATES, POSITIONS], F32, name=f"table_{axis}")
             nc.sync.dma_start(table[:], theta[k * GATES : (k + 1) * GATES, :])
             tables.append(table)
+        table_x, table_y, table_z = tables
 
-        quarter_turn = held.tile([GATES, 1], F32, name="quarter_turn")
-        nc.vector.memset(quarter_turn[:], math.pi / 2)
+        shifts = {}
+        for name, value in (("cos", -math.pi / 2), ("plus", math.pi / 4), ("minus", -math.pi / 4)):
+            shifts[name] = held.tile([GATES, 1], F32, name=f"shift_{name}")
+            nc.vector.memset(shifts[name][:], value)
         warm = held.tile([GATES, 1], F32, name="warm")
-        nc.scalar.activation(warm[:], quarter_turn[:], SINE)
+        nc.scalar.activation(warm[:], shifts["plus"][:], SINE)
         identity = held.tile([GATES, GATES], F32, name="identity")
         make_identity(nc, identity[:])
+        scaled_identity = held.tile([GATES, GATES], F32, name="scaled_identity")
+        nc.vector.tensor_scalar(
+            out=scaled_identity[:], in0=identity[:], scalar1=math.sqrt(0.5), scalar2=None, op0=MULT
+        )
 
-        for j in range(LISTED // PIECE):
-            piece_offsets = offsets[:, j * (PIECE // 16) : (j + 1) * (PIECE // 16)]
+        picked_x = held.tile([GATES, LISTED], F32, name="picked_x")
+        nc.scalar.activation(picked_x[:], table_x[:].indirect(offsets[:]), COPY)
 
-            angles = trig.tile([GATES, 3, PIECE], F32, name="angles")
-            cos_sin = trig.tile([GATES, 3, 2, PIECE], F32, name="cos_sin")
-            for k, table in enumerate(tables):
-                nc.scalar.activation(angles[:, k, :], table[:].indirect(piece_offsets), COPY)
-                nc.scalar.activation(cos_sin[:, k, COS, :], angles[:, k, :], SINE, bias=quarter_turn[:], scale=0.5)
-                nc.scalar.activation(cos_sin[:, k, SIN, :], angles[:, k, :], SINE, scale=0.5)
-            of_x, of_y, of_z = cos_sin[:, 0], cos_sin[:, 1], cos_sin[:, 2]
+        angle_sums, angle_sizes = [], []
+        for c in range(LISTED // CHUNK):
+            picked_y = chunks.tile([GATES, CHUNK], F32, name="picked_y")
+            nc.scalar.activation(
+                picked_y[:], table_y[:].indirect(offsets[:, c * (CHUNK // 16) : (c + 1) * (CHUNK // 16)]), COPY
+            )
+            x_chunk = picked_x[:, c * CHUNK : (c + 1) * CHUNK]
+            sums = chunks.tile([GATES, 2, CHUNK], F32, name="sums")
+            nc.vector.tensor_tensor(sums[:, SUM, :], x_chunk, picked_y[:], ADD)
+            nc.vector.tensor_tensor(sums[:, DIFFERENCE, :], x_chunk, picked_y[:], SUBTRACT)
+            sizes = chunks.tile([GATES, 2, CHUNK], F32, name="sizes")
+            nc.vector.tensor_scalar(
+                out=sizes[:].bitcast(I32), in0=sums[:].bitcast(I32), scalar1=ALL_BUT_SIGN, scalar2=None, op0=BIT_AND
+            )
+            angle_sums.append(sums)
+            angle_sizes.append(sizes)
 
-            xy = work.tile([GATES, 2, 2, PIECE], F32, name="xy")
-            for x in (COS, SIN):
-                x_bank = banks.tile([GATES, PIECE], F32, name=f"x_bank{x}")
-                nc.tensor.matmul(x_bank[:], identity[:], of_x[:, x, :], start=True, stop=True)
+        for j in range(PIECES):
+            c, inside = divmod(j * PIECE, CHUNK)
+
+            picked_z = ahead.tile([GATES, PIECE], F32, name="picked_z")
+            nc.scalar.activation(
+                picked_z[:], table_z[:].indirect(offsets[:, j * (PIECE // 16) : (j + 1) * (PIECE // 16)]), COPY
+            )
+            of_z = ahead.tile([GATES, 2, PIECE], F32, name="of_z")
+            z_bank = banks.tile([GATES, 2, PIECE], F32, name="z_bank")
+            for s, shift in ((PLUS, shifts["plus"]), (MINUS, shifts["minus"])):
+                nc.scalar.activation(of_z[:, s, :], picked_z[:], SINE, bias=shift[:], scale=0.5)
+                nc.tensor.matmul(z_bank[:, s, :], scaled_identity[:], of_z[:, s, :], start=True, stop=True)
+
+            cosines = ahead.tile([GATES, 2, PIECE], F32, name="cosines")
+            nc.scalar.activation(
+                cosines[:], angle_sizes[c][:, :, inside : inside + PIECE], SINE, bias=shifts["cos"][:], scale=0.5
+            )
+            sines = ahead.tile([GATES, 2, PIECE], F32, name="sines")
+            nc.scalar.activation(sines[:], angle_sums[c][:, :, inside : inside + PIECE], SINE, scale=0.5)
+
+            products = work.tile([GATES, 2, 2, 2, PIECE], F32, name="products")
+            for g, of_sums in ((COS, cosines), (SIN, sines)):
                 nc.vector.tensor_tensor(
-                    xy[:, x, :, :], x_bank[:].unsqueeze(1).to_broadcast([GATES, 2, PIECE]), of_y, MULT
-                )
-            zxy = work.tile([GATES, 2, 2, 2, PIECE], F32, name="zxy")
-            for z in (COS, SIN):
-                z_bank = banks.tile([GATES, PIECE], F32, name=f"z_bank{z}")
-                nc.tensor.matmul(z_bank[:], identity[:], of_z[:, z, :], start=True, stop=True)
-                nc.vector.tensor_tensor(
-                    zxy[:, z, :, :, :].rearrange("p x y w -> p (x y) w"),
-                    z_bank[:].unsqueeze(1).to_broadcast([GATES, 4, PIECE]),
-                    xy[:].rearrange("p x y w -> p (x y) w"),
+                    products[:, g],
+                    z_bank[:].unsqueeze(2).to_broadcast([GATES, 2, 2, PIECE]),
+                    of_sums[:].unsqueeze(1).to_broadcast([GATES, 2, 2, PIECE]),
                     MULT,
                 )
 
-            adder = nc.vector if j == LISTED // PIECE - 1 else nc.gpsimd
-            blocks = (
-                (zxy[:, COS, COS, COS, :], ADD, zxy[:, SIN, SIN, SIN, :]),
-                (zxy[:, COS, SIN, SIN, :], SUBTRACT, zxy[:, SIN, COS, COS, :]),
-                (zxy[:, COS, COS, SIN, :], ADD, zxy[:, SIN, SIN, COS, :]),
-                (zxy[:, SIN, COS, SIN, :], SUBTRACT, zxy[:, COS, SIN, COS, :]),
+            adder = nc.vector if j >= PIECES - VECTOR_ADDS else nc.gpsimd
+            blocks = work.tile([GATES, 4, PIECE], F32, name="blocks")
+            adder.tensor_tensor(
+                blocks[:, 0::3, :], products[:, :, MINUS, SUM, :], products[:, :, PLUS, DIFFERENCE, :], SUBTRACT
             )
-            for q, (first, op, second) in enumerate(blocks):
-                block = work.tile([GATES, PIECE], F32, name=f"block{q}")
-                adder.tensor_tensor(block[:], first, second, op)
-                nc.sync.dma_start(out[q * GATES : (q + 1) * GATES, j * PIECE : (j + 1) * PIECE], block[:])
+            adder.tensor_tensor(
+                blocks[:, 1:3, :], products[:, :, PLUS, SUM, :], products[:, :, MINUS, DIFFERENCE, :], ADD
+            )
+            nc.sync.dma_start(out_blocks[:, :, j * PIECE : (j + 1) * PIECE], blocks[:])

@@ -18,7 +18,7 @@ POSITIONS = 4096
 LISTED = 2048
 CHUNK = 512
 PIECE = 256
-PIECES = LISTED // PIECE
+WIDTHS = (PIECE // 2, PIECE // 2) + (PIECE,) * (LISTED // PIECE - 1)
 VECTOR_ADDS = 2
 ALL_BUT_SIGN = 0x7FFFFFFF
 SUM, DIFFERENCE = 0, 1
@@ -80,41 +80,42 @@ def tile_quantumlearnablepositionalencoding_kernel(tc, theta, offs, out):
             angle_sums.append(sums)
             angle_sizes.append(sizes)
 
-        for j in range(PIECES):
-            c, inside = divmod(j * PIECE, CHUNK)
+        for j, width in enumerate(WIDTHS):
+            first = sum(WIDTHS[:j])
+            c, inside = divmod(first, CHUNK)
 
-            picked_z = ahead.tile([GATES, PIECE], F32, name="picked_z")
+            picked_z = ahead.tile([GATES, width], F32, name="picked_z")
             nc.scalar.activation(
-                picked_z[:], table_z[:].indirect(offsets[:, j * (PIECE // 16) : (j + 1) * (PIECE // 16)]), COPY
+                picked_z[:], table_z[:].indirect(offsets[:, first // 16 : (first + width) // 16]), COPY
             )
-            of_z = ahead.tile([GATES, 2, PIECE], F32, name="of_z")
-            z_bank = banks.tile([GATES, 2, PIECE], F32, name="z_bank")
+            of_z = ahead.tile([GATES, 2, width], F32, name="of_z")
+            z_bank = banks.tile([GATES, 2, width], F32, name="z_bank")
             for s, shift in ((PLUS, shifts["plus"]), (MINUS, shifts["minus"])):
                 nc.scalar.activation(of_z[:, s, :], picked_z[:], SINE, bias=shift[:], scale=0.5)
                 nc.tensor.matmul(z_bank[:, s, :], scaled_identity[:], of_z[:, s, :], start=True, stop=True)
 
-            cosines = ahead.tile([GATES, 2, PIECE], F32, name="cosines")
+            cosines = ahead.tile([GATES, 2, width], F32, name="cosines")
             nc.scalar.activation(
-                cosines[:], angle_sizes[c][:, :, inside : inside + PIECE], SINE, bias=shifts["cos"][:], scale=0.5
+                cosines[:], angle_sizes[c][:, :, inside : inside + width], SINE, bias=shifts["cos"][:], scale=0.5
             )
-            sines = ahead.tile([GATES, 2, PIECE], F32, name="sines")
-            nc.scalar.activation(sines[:], angle_sums[c][:, :, inside : inside + PIECE], SINE, scale=0.5)
+            sines = ahead.tile([GATES, 2, width], F32, name="sines")
+            nc.scalar.activation(sines[:], angle_sums[c][:, :, inside : inside + width], SINE, scale=0.5)
 
-            products = work.tile([GATES, 2, 2, 2, PIECE], F32, name="products")
+            products = work.tile([GATES, 2, 2, 2, width], F32, name="products")
             for g, of_sums in ((COS, cosines), (SIN, sines)):
                 nc.vector.tensor_tensor(
                     products[:, g],
-                    z_bank[:].unsqueeze(2).to_broadcast([GATES, 2, 2, PIECE]),
-                    of_sums[:].unsqueeze(1).to_broadcast([GATES, 2, 2, PIECE]),
+                    z_bank[:].unsqueeze(2).to_broadcast([GATES, 2, 2, width]),
+                    of_sums[:].unsqueeze(1).to_broadcast([GATES, 2, 2, width]),
                     MULT,
                 )
 
-            adder = nc.vector if j >= PIECES - VECTOR_ADDS else nc.gpsimd
-            blocks = work.tile([GATES, 4, PIECE], F32, name="blocks")
+            adder = nc.vector if j >= len(WIDTHS) - VECTOR_ADDS else nc.gpsimd
+            blocks = work.tile([GATES, 4, width], F32, name="blocks")
             adder.tensor_tensor(
                 blocks[:, 0::3, :], products[:, :, MINUS, SUM, :], products[:, :, PLUS, DIFFERENCE, :], SUBTRACT
             )
             adder.tensor_tensor(
                 blocks[:, 1:3, :], products[:, :, PLUS, SUM, :], products[:, :, MINUS, DIFFERENCE, :], ADD
             )
-            nc.sync.dma_start(out_blocks[:, :, j * PIECE : (j + 1) * PIECE], blocks[:])
+            nc.sync.dma_start(out_blocks[:, :, first : first + width], blocks[:])

@@ -19,10 +19,8 @@ LISTED = 2048
 CHUNK = 512
 PIECE = 256
 WIDTHS = (PIECE // 2, PIECE // 2) + (PIECE,) * (LISTED // PIECE - 1)
-VECTOR_ADDS = 2
+VECTOR_ADDS = 1
 ALL_BUT_SIGN = 0x7FFFFFFF
-SUM, DIFFERENCE = 0, 1
-COS, SIN = 0, 1
 PLUS, MINUS = 0, 1
 
 
@@ -34,6 +32,7 @@ def tile_quantumlearnablepositionalencoding_kernel(tc, theta, offs, out):
         tc.tile_pool(name="held", bufs=1) as held,
         tc.tile_pool(name="chunks", bufs=LISTED // CHUNK) as chunks,
         tc.tile_pool(name="ahead", bufs=2) as ahead,
+        tc.tile_pool(name="sines", bufs=3) as sines,
         tc.tile_pool(name="work", bufs=3) as work,
         tc.psum_pool(name="banks", bufs=4) as banks,
     ):
@@ -63,22 +62,25 @@ def tile_quantumlearnablepositionalencoding_kernel(tc, theta, offs, out):
         picked_x = held.tile([GATES, LISTED], F32, name="picked_x")
         nc.scalar.activation(picked_x[:], table_x[:].indirect(offsets[:]), COPY)
 
-        angle_sums, angle_sizes = [], []
+        angle_rows = []
         for c in range(LISTED // CHUNK):
             picked_y = chunks.tile([GATES, CHUNK], F32, name="picked_y")
             nc.scalar.activation(
                 picked_y[:], table_y[:].indirect(offsets[:, c * (CHUNK // 16) : (c + 1) * (CHUNK // 16)]), COPY
             )
             x_chunk = picked_x[:, c * CHUNK : (c + 1) * CHUNK]
-            sums = chunks.tile([GATES, 2, CHUNK], F32, name="sums")
-            nc.vector.tensor_tensor(sums[:, SUM, :], x_chunk, picked_y[:], ADD)
-            nc.vector.tensor_tensor(sums[:, DIFFERENCE, :], x_chunk, picked_y[:], SUBTRACT)
-            sizes = chunks.tile([GATES, 2, CHUNK], F32, name="sizes")
-            nc.vector.tensor_scalar(
-                out=sizes[:].bitcast(I32), in0=sums[:].bitcast(I32), scalar1=ALL_BUT_SIGN, scalar2=None, op0=BIT_AND
-            )
-            angle_sums.append(sums)
-            angle_sizes.append(sizes)
+            angles = chunks.tile([GATES, 4, CHUNK], F32, name="angles")
+            nc.vector.tensor_tensor(angles[:, 3, :], x_chunk, picked_y[:], ADD)
+            nc.vector.tensor_tensor(angles[:, 2, :], x_chunk, picked_y[:], SUBTRACT)
+            for size, signed in ((0, 3), (1, 2)):
+                nc.vector.tensor_scalar(
+                    out=angles[:, size, :].bitcast(I32),
+                    in0=angles[:, signed, :].bitcast(I32),
+                    scalar1=ALL_BUT_SIGN,
+                    scalar2=None,
+                    op0=BIT_AND,
+                )
+            angle_rows.append(angles)
 
         for j, width in enumerate(WIDTHS):
             first = sum(WIDTHS[:j])
@@ -94,28 +96,23 @@ def tile_quantumlearnablepositionalencoding_kernel(tc, theta, offs, out):
                 nc.scalar.activation(of_z[:, s, :], picked_z[:], SINE, bias=shift[:], scale=0.5)
                 nc.tensor.matmul(z_bank[:, s, :], scaled_identity[:], of_z[:, s, :], start=True, stop=True)
 
-            cosines = ahead.tile([GATES, 2, width], F32, name="cosines")
-            nc.scalar.activation(
-                cosines[:], angle_sizes[c][:, :, inside : inside + width], SINE, bias=shifts["cos"][:], scale=0.5
-            )
-            sines = ahead.tile([GATES, 2, width], F32, name="sines")
-            nc.scalar.activation(sines[:], angle_sums[c][:, :, inside : inside + width], SINE, scale=0.5)
+            trig = sines.tile([GATES, 4, width], F32, name="trig")
+            columns = slice(inside, inside + width)
+            nc.scalar.activation(trig[:, 0:2, :], angle_rows[c][:, 0:2, columns], SINE, bias=shifts["cos"][:], scale=0.5)
+            nc.scalar.activation(trig[:, 2:4, :], angle_rows[c][:, 2:4, columns], SINE, scale=0.5)
 
-            products = work.tile([GATES, 2, 2, 2, width], F32, name="products")
-            for g, of_sums in ((COS, cosines), (SIN, sines)):
-                nc.vector.tensor_tensor(
-                    products[:, g],
-                    z_bank[:].unsqueeze(2).to_broadcast([GATES, 2, 2, width]),
-                    of_sums[:].unsqueeze(1).to_broadcast([GATES, 2, 2, width]),
-                    MULT,
-                )
+            first_terms = work.tile([GATES, 4, width], F32, name="first_terms")
+            nc.vector.tensor_tensor(
+                first_terms[:], z_bank[:, MINUS, :].unsqueeze(1).to_broadcast([GATES, 4, width]), trig[:], MULT
+            )
+            k_z_plus = z_bank[:, PLUS, :].unsqueeze(1).to_broadcast([GATES, 2, width])
+            second_terms = work.tile([GATES, 4, width], F32, name="second_terms")
+            nc.vector.tensor_tensor(second_terms[:, 1:3, :], k_z_plus, trig[:, 0::3, :], MULT)
+            nc.vector.scalar_tensor_tensor(
+                out=second_terms[:, 0::3, :], in0=k_z_plus, scalar=-1.0, in1=trig[:, 1:3, :], op0=MULT, op1=MULT
+            )
 
             adder = nc.vector if j >= len(WIDTHS) - VECTOR_ADDS else nc.gpsimd
             blocks = work.tile([GATES, 4, width], F32, name="blocks")
-            adder.tensor_tensor(
-                blocks[:, 0::3, :], products[:, :, MINUS, SUM, :], products[:, :, PLUS, DIFFERENCE, :], SUBTRACT
-            )
-            adder.tensor_tensor(
-                blocks[:, 1:3, :], products[:, :, PLUS, SUM, :], products[:, :, MINUS, DIFFERENCE, :], ADD
-            )
+            adder.tensor_tensor(blocks[:], first_terms[:], second_terms[:], ADD)
             nc.sync.dma_start(out_blocks[:, :, first : first + width], blocks[:])

@@ -91,10 +91,10 @@ def tile_quantumlearnablepositionalencoding_kernel(tc, theta, offs, out):
                 picked_z[:], table_z[:].indirect(offsets[:, first // 16 : (first + width) // 16]), COPY
             )
             of_z = ahead.tile([GATES, 2, width], F32, name="of_z")
-            z_bank = banks.tile([GATES, 2, width], F32, name="z_bank")
-            for s, shift in ((PLUS, shifts["plus"]), (MINUS, shifts["minus"])):
+            z_banks = [banks.tile([GATES, width], F32, name=f"z_bank_{s}") for s in (PLUS, MINUS)]
+            for s, shift in ((MINUS, shifts["minus"]), (PLUS, shifts["plus"])):
                 nc.scalar.activation(of_z[:, s, :], picked_z[:], SINE, bias=shift[:], scale=0.5)
-                nc.tensor.matmul(z_bank[:, s, :], scaled_identity[:], of_z[:, s, :], start=True, stop=True)
+                nc.tensor.matmul(z_banks[s][:], scaled_identity[:], of_z[:, s, :], start=True, stop=True)
 
             trig = sines.tile([GATES, 4, width], F32, name="trig")
             columns = slice(inside, inside + width)
@@ -103,9 +103,9 @@ def tile_quantumlearnablepositionalencoding_kernel(tc, theta, offs, out):
 
             first_terms = work.tile([GATES, 4, width], F32, name="first_terms")
             nc.vector.tensor_tensor(
-                first_terms[:], z_bank[:, MINUS, :].unsqueeze(1).to_broadcast([GATES, 4, width]), trig[:], MULT
+                first_terms[:], z_banks[MINUS][:].unsqueeze(1).to_broadcast([GATES, 4, width]), trig[:], MULT
             )
-            k_z_plus = z_bank[:, PLUS, :].unsqueeze(1).to_broadcast([GATES, 2, width])
+            k_z_plus = z_banks[PLUS][:].unsqueeze(1).to_broadcast([GATES, 2, width])
             second_terms = work.tile([GATES, 4, width], F32, name="second_terms")
             nc.vector.tensor_tensor(second_terms[:, 1:3, :], k_z_plus, trig[:, 0::3, :], MULT)
             nc.vector.scalar_tensor_tensor(

@@ -22,6 +22,7 @@ WIDTHS = (PIECE // 2, PIECE // 2) + (PIECE,) * (LISTED // PIECE - 1)
 VECTOR_ADDS = 1
 ALL_BUT_SIGN = 0x7FFFFFFF
 PLUS, MINUS = 0, 1
+K = math.sqrt(0.5)
 
 
 def tile_quantumlearnablepositionalencoding_kernel(tc, theta, offs, out):
@@ -54,10 +55,6 @@ def tile_quantumlearnablepositionalencoding_kernel(tc, theta, offs, out):
         nc.scalar.activation(warm[:], shifts["plus"][:], SINE)
         identity = held.tile([GATES, GATES], F32, name="identity")
         make_identity(nc, identity[:])
-        scaled_identity = held.tile([GATES, GATES], F32, name="scaled_identity")
-        nc.vector.tensor_scalar(
-            out=scaled_identity[:], in0=identity[:], scalar1=math.sqrt(0.5), scalar2=None, op0=MULT
-        )
 
         picked_x = held.tile([GATES, LISTED], F32, name="picked_x")
         nc.scalar.activation(picked_x[:], table_x[:].indirect(offsets[:]), COPY)
@@ -90,11 +87,14 @@ def tile_quantumlearnablepositionalencoding_kernel(tc, theta, offs, out):
             nc.scalar.activation(
                 picked_z[:], table_z[:].indirect(offsets[:, first // 16 : (first + width) // 16]), COPY
             )
-            of_z = ahead.tile([GATES, 2, width], F32, name="of_z")
-            z_banks = [banks.tile([GATES, width], F32, name=f"z_bank_{s}") for s in (PLUS, MINUS)]
+            of_z = sines.tile([GATES, 2, width], F32, name="of_z")
+            z_rows = [of_z[:, s, :] for s in (PLUS, MINUS)]
             for s, shift in ((MINUS, shifts["minus"]), (PLUS, shifts["plus"])):
                 nc.scalar.activation(of_z[:, s, :], picked_z[:], SINE, bias=shift[:], scale=0.5)
-                nc.tensor.matmul(z_banks[s][:], scaled_identity[:], of_z[:, s, :], start=True, stop=True)
+                if j > 0:
+                    z_bank = banks.tile([GATES, width], F32, name=f"z_bank_{s}")
+                    nc.tensor.matmul(z_bank[:], identity[:], of_z[:, s, :], start=True, stop=True)
+                    z_rows[s] = z_bank[:]
 
             trig = sines.tile([GATES, 4, width], F32, name="trig")
             columns = slice(inside, inside + width)
@@ -102,14 +102,21 @@ def tile_quantumlearnablepositionalencoding_kernel(tc, theta, offs, out):
             nc.scalar.activation(trig[:, 2:4, :], angle_rows[c][:, 2:4, columns], SINE, scale=0.5)
 
             first_terms = work.tile([GATES, 4, width], F32, name="first_terms")
-            nc.vector.tensor_tensor(
-                first_terms[:], z_banks[MINUS][:].unsqueeze(1).to_broadcast([GATES, 4, width]), trig[:], MULT
-            )
-            k_z_plus = z_banks[PLUS][:].unsqueeze(1).to_broadcast([GATES, 2, width])
-            second_terms = work.tile([GATES, 4, width], F32, name="second_terms")
-            nc.vector.tensor_tensor(second_terms[:, 1:3, :], k_z_plus, trig[:, 0::3, :], MULT)
             nc.vector.scalar_tensor_tensor(
-                out=second_terms[:, 0::3, :], in0=k_z_plus, scalar=-1.0, in1=trig[:, 1:3, :], op0=MULT, op1=MULT
+                out=first_terms[:],
+                in0=z_rows[MINUS].unsqueeze(1).to_broadcast([GATES, 4, width]),
+                scalar=K,
+                in1=trig[:],
+                op0=MULT,
+                op1=MULT,
+            )
+            z_plus = z_rows[PLUS].unsqueeze(1).to_broadcast([GATES, 2, width])
+            second_terms = work.tile([GATES, 4, width], F32, name="second_terms")
+            nc.vector.scalar_tensor_tensor(
+                out=second_terms[:, 1:3, :], in0=z_plus, scalar=K, in1=trig[:, 0::3, :], op0=MULT, op1=MULT
+            )
+            nc.vector.scalar_tensor_tensor(
+                out=second_terms[:, 0::3, :], in0=z_plus, scalar=-K, in1=trig[:, 1:3, :], op0=MULT, op1=MULT
             )
 
             adder = nc.vector if j >= len(WIDTHS) - VECTOR_ADDS else nc.gpsimd

@@ -61,7 +61,10 @@ def tile_quantumlearnablepositionalencoding_kernel(tc, theta, offs, out):
 
         angle_rows = []
         for c in range(LISTED // CHUNK):
-            picked_y = chunks.tile([GATES, CHUNK], F32, name="picked_y")
+            if c < LISTED // CHUNK - 1:
+                picked_y = chunks.tile([GATES, CHUNK], F32, name="picked_y")
+            else:
+                picked_y = sines.tile([GATES, CHUNK], F32, name="picked_y_last", tag="trig")
             nc.scalar.activation(
                 picked_y[:], table_y[:].indirect(offsets[:, c * (CHUNK // 16) : (c + 1) * (CHUNK // 16)]), COPY
             )

import math

import concourse.mybir as mybir
from concourse.masks import make_identity

F32 = mybir.dt.float32
I32 = mybir.dt.int32
U16 = mybir.dt.uint16
COPY = mybir.ActivationFunctionType.Copy
SINE = mybir.ActivationFunctionType.Sin
MULT = mybir.AluOpType.mult
ADD = mybir.AluOpType.add
SUBTRACT = mybir.AluOpType.subtract
BIT_AND = mybir.AluOpType.bitwise_and

GATES = 128
POSITIONS = 4096
LISTED = 2048
CHUNK = 512
PIECE = 256
WIDTHS = (PIECE // 2, PIECE // 2) + (PIECE,) * (LISTED // PIECE - 1)
VECTOR_ADDS = 1
ALL_BUT_SIGN = 0x7FFFFFFF
PLUS, MINUS = 0, 1
K = math.sqrt(0.5)


def tile_quantumlearnablepositionalencoding_kernel(tc, theta, offs, out):
    nc = tc.nc
    out_blocks = out.rearrange("(q r) n -> r q n", q=4)

    with (
        tc.tile_pool(name="held", bufs=1) as held,
        tc.tile_pool(name="chunks", bufs=LISTED // CHUNK) as chunks,
        tc.tile_pool(name="ahead", bufs=2) as ahead,
        tc.tile_pool(name="sines", bufs=3) as sines,
        tc.tile_pool(name="work", bufs=3) as work,
        tc.psum_pool(name="banks", bufs=4) as banks,
    ):
        offsets = held.tile([GATES, LISTED // 16], U16, name="offsets")
        nc.sync.dma_start(offsets[:], offs)

        tables = []
        for k, axis in enumerate("xyz"):
            table = held.tile([GATES, POSITIONS], F32, name=f"table_{axis}")
            nc.sync.dma_start(table[:], theta[k * GATES : (k + 1) * GATES, :])
            tables.append(table)
        table_x, table_y, table_z = tables

        shifts = {}
        for name, value in (("cos", -math.pi / 2), ("plus", math.pi / 4), ("minus", -math.pi / 4)):
            shifts[name] = held.tile([GATES, 1], F32, name=f"shift_{name}")
            nc.vector.memset(shifts[name][:], value)
        warm = held.tile([GATES, 1], F32, name="warm")
        nc.scalar.activation(warm[:], shifts["plus"][:], SINE)
        identity = held.tile([GATES, GATES], F32, name="identity")
        make_identity(nc, identity[:])

        picked_x = held.tile([GATES, LISTED], F32, name="picked_x")
        nc.scalar.activation(picked_x[:], table_x[:].indirect(offsets[:]), COPY)

        angle_rows = []
        for c in range(LISTED // CHUNK):
            if c < LISTED // CHUNK - 1:
                picked_y = chunks.tile([GATES, CHUNK], F32, name="picked_y")
            else:
                picked_y = sines.tile([GATES, CHUNK], F32, name="picked_y_last", tag="trig")
            nc.scalar.activation(
                picked_y[:], table_y[:].indirect(offsets[:, c * (CHUNK // 16) : (c + 1) * (CHUNK // 16)]), COPY
            )
            x_chunk = picked_x[:, c * CHUNK : (c + 1) * CHUNK]
            angles = chunks.tile([GATES, 4, CHUNK], F32, name="angles")
            nc.vector.tensor_tensor(angles[:, 3, :], x_chunk, picked_y[:], ADD)
            nc.vector.tensor_tensor(angles[:, 2, :], x_chunk, picked_y[:], SUBTRACT)
            for size, signed in ((0, 3), (1, 2)):
                nc.vector.tensor_scalar(
                    out=angles[:, size, :].bitcast(I32),
                    in0=angles[:, signed, :].bitcast(I32),
                    scalar1=ALL_BUT_SIGN,
                    scalar2=None,
                    op0=BIT_AND,
                )
            angle_rows.append(angles)

        for j, width in enumerate(WIDTHS):
            first = sum(WIDTHS[:j])
            c, inside = divmod(first, CHUNK)

            picked_z = ahead.tile([GATES, width], F32, name="picked_z")
            nc.scalar.activation(
                picked_z[:], table_z[:].indirect(offsets[:, first // 16 : (first + width) // 16]), COPY
            )
            of_z = sines.tile([GATES, 2, width], F32, name="of_z")
            z_rows = [of_z[:, s, :] for s in (PLUS, MINUS)]
            for s, shift in ((MINUS, shifts["minus"]), (PLUS, shifts["plus"])):
                nc.scalar.activation(of_z[:, s, :], picked_z[:], SINE, bias=shift[:], scale=0.5)
                if j > 0:
                    z_bank = banks.tile([GATES, width], F32, name=f"z_bank_{s}")
                    nc.tensor.matmul(z_bank[:], identity[:], of_z[:, s, :], start=True, stop=True)
                    z_rows[s] = z_bank[:]

            trig = sines.tile([GATES, 4, width], F32, name="trig")
            columns = slice(inside, inside + width)
            nc.scalar.activation(trig[:, 0:2, :], angle_rows[c][:, 0:2, columns], SINE, bias=shifts["cos"][:], scale=0.5)
            nc.scalar.activation(trig[:, 2:4, :], angle_rows[c][:, 2:4, columns], SINE, scale=0.5)

            first_terms = work.tile([GATES, 4, width], F32, name="first_terms")
            nc.vector.scalar_tensor_tensor(
                out=first_terms[:],
                in0=z_rows[MINUS].unsqueeze(1).to_broadcast([GATES, 4, width]),
                scalar=K,
                in1=trig[:],
                op0=MULT,
                op1=MULT,
            )
            z_plus = z_rows[PLUS].unsqueeze(1).to_broadcast([GATES, 2, width])
            second_terms = work.tile([GATES, 4, width], F32, name="second_terms")
            nc.vector.scalar_tensor_tensor(
                out=second_terms[:, 1:3, :], in0=z_plus, scalar=K, in1=trig[:, 0::3, :], op0=MULT, op1=MULT
            )
            nc.vector.scalar_tensor_tensor(
                out=second_terms[:, 0::3, :], in0=z_plus, scalar=-K, in1=trig[:, 1:3, :], op0=MULT, op1=MULT
            )

            adder = nc.vector if j >= len(WIDTHS) - VECTOR_ADDS else nc.gpsimd
            blocks = work.tile([GATES, 4, width], F32, name="blocks")
            adder.tensor_tensor(blocks[:], first_terms[:], second_terms[:], ADD)
            nc.sync.dma_start(out_blocks[:, :, first : first + width], blocks[:])
